import numpy as np
import ml_dtypes


def mxq(x, axis, fmt="e4m3"):
    dtype, down = {"e4m3": (ml_dtypes.float8_e4m3fn, 7), "e5m2": (ml_dtypes.float8_e5m2, 14)}[fmt]
    v = np.moveaxis(np.asarray(x, np.float32).astype(ml_dtypes.bfloat16).astype(np.float64), axis, -1)
    blocks = v.reshape(v.shape[:-1] + (-1, 32))
    amax = np.abs(blocks).max(-1, keepdims=True)
    byte = np.maximum(np.where(amax > 0, np.frexp(amax)[1] - 1 + 127, 0) - down, 1)
    scale = np.exp2(byte - 127.0)
    codes = (blocks / scale).astype(np.float32).astype(dtype).astype(np.float64)
    return np.moveaxis((codes * scale).reshape(v.shape), -1, axis)


WIDE = False


def mx_kscale(k):
    if not WIDE:
        return np.ones(k)
    levels = np.array([10, -10, 5, -5, 0])
    if k % 512:
        return np.exp2(np.random.permutation(np.resize(levels, k // 32))).repeat(32)
    a = np.empty((k // 512, 16))
    for p in range(k // 512):
        a[p, :8] = np.random.permutation(np.resize(levels, 8))
        for g in range(8):
            far = levels[np.abs(levels - a[p, g]) >= 10]
            a[p, g + 8] = far[np.random.randint(len(far))]
    return np.exp2(a.ravel()).repeat(32)


BF16 = ml_dtypes.bfloat16


def bf(x):
    return np.asarray(x, np.float32).astype(BF16)


def f64(x):
    return np.asarray(x).astype(np.float64)


B, T, G, I, H = 4, 256, 8, 512, 512


def draw0():
    s = mx_kscale(I)
    return {"x": bf((np.random.standard_normal((B, T, G, I)) * s).reshape(B, T, G * I)),
            "W": bf(np.random.standard_normal((G, H, I)) / np.sqrt(I) / s),
            "b": bf(np.random.standard_normal((G, H)) * 0.5)}


def core(x, W, b):
    xg = f64(x).reshape(B, T, G, I)
    xq = mxq(xg, 3, "e4m3")
    wq = mxq(f64(W), 2, "e4m3")
    y = xq.transpose(2, 0, 1, 3).reshape(G, B * T, I) @ wq.transpose(0, 2, 1)
    out = y.reshape(G, B, T, H).transpose(1, 2, 0, 3) + f64(b)
    return np.swapaxes(out, -1, -2).reshape(B, T, G * H)


def e4m3fn_bytes(y):
    return np.clip(np.asarray(y, np.float64), -448.0, 448.0).astype(np.float32).astype(ml_dtypes.float8_e4m3fn).view(np.uint8)


def e4m3fn_values(b):
    return np.asarray(b, np.uint8).view(ml_dtypes.float8_e4m3fn).astype(np.float64)


def setup_inputs():
    d = draw0()
    x0 = np.asarray(d['x']).astype(np.float64)
    s = (np.max(np.abs(x0), axis=(0, 1), keepdims=True) / 448.0).astype(np.float32)
    out = {}
    for k, v in d.items():
        if k == 'x':
            out['x_bytes'] = e4m3fn_bytes(x0 / s.astype(np.float64))
            out['x_scale'] = s
        else:
            out[k] = v
    return out


def reference(x_bytes, x_scale, W, b):
    return core(e4m3fn_values(x_bytes) * x_scale.astype(np.float64), W, b)

@@ -1,0 +1,263 @@
+from contextlib import ExitStack
+
+import concourse.mybir as mybir
+from concourse.masks import make_identity
+
+F32 = mybir.dt.float32
+BF16 = mybir.dt.bfloat16
+U32 = mybir.dt.uint32
+U8 = mybir.dt.uint8
+FP8 = mybir.dt.float8_e4m3fn
+FP8X4 = mybir.dt.float8_e4m3fn_x4
+MULT = mybir.AluOpType.mult
+ADD = mybir.AluOpType.add
+IDENT = mybir.ActivationFunctionType.Identity
+
+P = 128
+NTOK = 1024
+G = 8
+I = 512
+H = 512
+NT = NTOK // P
+HC = H // P
+NPAIR = NT // 2
+NCH = 2 * NT
+HALF = 4 * I
+
+FLOPS = 2 * NTOK * G * I * H
+
+WT0 = 1
+W_ORDER = (4, 5, 6, 7, 0, 1, 2, 3)
+
+
+def long_way(q, gh, c):
+    return gh == 1
+
+
+def second_copy_on_vector(q, c, t):
+    return False
+
+
+def tile_groupedlinear_kernel(tc, x_bytes, x_scale, W, b, out):
+    nc = tc.nc
+    xb_flat = x_bytes.flatten_outer_dims()
+    out_flat = out.flatten_outer_dims()
+    scale_row = x_scale.rearrange("a b k -> (a b k)")
+
+    with ExitStack() as ctx:
+        const = ctx.enter_context(tc.tile_pool(name="const", bufs=1))
+        xin = ctx.enter_context(tc.tile_pool(name="xin", bufs=8))
+        work = ctx.enter_context(tc.tile_pool(name="work", bufs=3))
+        codes = ctx.enter_context(tc.tile_pool(name="codes", bufs=4))
+        outp = ctx.enter_context(tc.tile_pool(name="outp", bufs=8))
+        tps = ctx.enter_context(tc.psum_pool(name="tps", bufs=2))
+        accs = ctx.enter_context(tc.psum_pool(name="accs", bufs=4))
+        bts = ctx.enter_context(tc.psum_pool(name="bts", bufs=2))
+        ctx.enter_context(tc.manual_schedule(engines={mybir.EngineType.PE}))
+
+        srow = const.tile([P, P], F32, name="srow")
+        nc.gpsimd.memset(srow[:], 0.0)
+        nc.sync.dma_start(out=srow[0:G * I // P, :], in_=scale_row.rearrange("(j i) -> j i", i=P))
+        ident = const.tile([P, P], F32, name="ident")
+        make_identity(nc, ident[:])
+        brow = const.tile([P, P], BF16, name="brow")
+        nc.gpsimd.memset(brow[:], 0.0)
+        nc.scalar.dma_start(out=brow[0:G * HC, :], in_=b.rearrange("g (c p) -> (g c) p", p=P))
+        ident_bf = const.tile([P, P], BF16, name="ident_bf")
+        make_identity(nc, ident_bf[:])
+
+        xbytes = []
+        for i in range(NT):
+            xbytes.append(xin.tile([P, G * I], U8, name="xbytes%d" % i, tag="xbytes"))
+        scale_bc = const.tile([P, G * I], F32, name="scale_bc")
+        w_raw = const.tile([P, G, HC, I], BF16, name="w_raw")
+        for i in range(2):
+            nc.sync.dma_start(out=xbytes[i][:, HALF:2 * HALF], in_=xb_flat[i * P:(i + 1) * P, HALF:2 * HALF])
+        for i in range(2):
+            nc.sync.dma_start(out=xbytes[i][:, 0:HALF], in_=xb_flat[i * P:(i + 1) * P, 0:HALF])
+        for g in W_ORDER:
+            nc.sync.dma_start(out=w_raw[:, g], in_=W[g].rearrange("(c p) k -> p c k", p=P))
+        for i in range(2, NT):
+            nc.sync.dma_start(out=xbytes[i][:], in_=xb_flat[i * P:(i + 1) * P, :])
+
+        w_codes = const.tile([P, G, H], U32, name="w_codes", align_bytes=64)
+        w_scales = const.tile([P, G, H], U8, name="w_scales", align_bytes=64)
+        bias_col = const.tile([P, G * HC], F32, name="bias_col")
+        bias_blk = const.tile([P, 2, HC, P, 4], F32, name="bias_blk")
+
+        def prep_scale():
+            pst = tps.tile([P, P], F32, name="pst", tag="tp")
+            nc.tensor.transpose(pst[:], srow[:], ident[:])
+            scol = const.tile([P, G * I // P], F32, name="scol")
+            nc.vector.tensor_copy(out=scol[:], in_=pst[:, 0:G * I // P])
+            for n, bank in enumerate((4, 5, 6, 7, 0, 1, 2, 3)):
+                pbc = accs.tile([P, 4, P], F32, name="pbc", tag="acc")
+                for j in range(4 * bank, 4 * bank + 4):
+                    nc.tensor.transpose(pbc[:, j % 4, :], scol[:, j:j + 1].to_broadcast([P, P]), ident[:])
+                dst = scale_bc[:, bank * I:(bank + 1) * I]
+                if n in (0, 1):
+                    nc.vector.tensor_copy(out=dst, in_=pbc[:].rearrange("p q n -> p (q n)"))
+                else:
+                    nc.scalar.copy(out=dst, in_=pbc[:].rearrange("p q n -> p (q n)"))
+
+        def prep_bias_col():
+            pb = tps.tile([P, P], BF16, name="pb", tag="tp")
+            nc.tensor.transpose(pb[:], brow[:], ident_bf[:])
+            nc.scalar.copy(out=bias_col[:], in_=pb[:, 0:G * HC])
+
+        def prep_bias_blk(gh, c):
+            ps = accs.tile([P, 4, P], F32, name="ps", tag="acc")
+            for a in range(4):
+                row = (4 * gh + a) * HC + c
+                nc.tensor.matmul(out=ps[:, a, :], lhsT=ident_bf[:, row:row + 1].to_broadcast([P, P]), rhs=brow[:],
+                                 start=True, stop=True)
+            nc.scalar.copy(out=bias_blk[:, gh, c], in_=ps[:].rearrange("p a h -> p h a"))
+
+        def widen(k):
+            q, r = k // 4, k % 4
+            i, gh = 2 * q + r % 2, 1 - r // 2
+            xb = work.tile([P, HALF], BF16, name="xb", tag="xb")
+            pieces = 2 if k == 0 else 1
+            w = HALF // pieces
+            for n in range(pieces):
+                cs = slice(gh * HALF + n * w, gh * HALF + (n + 1) * w)
+                nc.vector.tensor_tensor(out=xb[:, n * w:(n + 1) * w], in0=xbytes[i][:, cs].bitcast(FP8),
+                                        in1=scale_bc[:, cs], op=MULT)
+            return xb
+
+        def turn(words, dst_words):
+            for j in range(2):
+                tp = tps.tile([P, 2, 2, P], F32, name="tp", tag="tp")
+                for a in range(2):
+                    n = 2 * j + a
+                    for u in range(2):
+                        nc.tensor.transpose(tp[:, a, u, :], words[:, 256 * n + u:256 * (n + 1):2], ident[:])
+                nc.scalar.copy(out=dst_words[:, 2 * j:2 * j + 2], in_=tp[:].rearrange("p a u r -> p a r u"))
+
+        def turn_x(xb, xg, t):
+            xg_words = xg[:].bitcast(F32).rearrange("p (a r u) -> p a r u", a=4, u=2)
+            turn(xb[:].bitcast(F32), xg_words[:, :, t * P:(t + 1) * P, :])
+
+        def quant_x(xg):
+            xc = codes.tile([P, 8 * P], U32, name="xc", tag="xc", align_bytes=64)
+            xs = codes.tile([P, 8 * P], U8, name="xs", tag="xs", align_bytes=64)
+            nc.vector.quantize_mx(out=xc[:].bitcast(FP8X4), scales=xs[:], in_=xg[:])
+            return xc, xs
+
+        def turn_w(g):
+            wg = work.tile([P, H * 4], BF16, name="wg", tag="wg", align_bytes=64, bufs=2)
+            turn(w_raw[:, g].rearrange("p c k -> p (c k)").bitcast(F32),
+                 wg[:].bitcast(F32).rearrange("p (a r u) -> p a r u", a=4, u=2))
+            return wg
+
+        def quant_w(g, wg):
+            nc.vector.quantize_mx(out=w_codes[:, g].bitcast(FP8X4), scales=w_scales[:, g], in_=wg[:])
+
+        osbs = {}
+
+        def osb_of(i, c):
+            if (i, c) not in osbs:
+                osbs[(i, c)] = [outp.tile([P, P, G], F32, name="osb", tag="osb"), 0]
+            return osbs[(i, c)]
+
+        def finish(i, c):
+            ent = osb_of(i, c)
+            ent[1] += 1
+            if ent[1] == 2:
+                nc.sync.dma_start(out=out_flat[i * P:(i + 1) * P, c * P * G:(c + 1) * P * G],
+                                  in_=ent[0][:].rearrange("p h g -> p (h g)"))
+
+        def unit_a(i, gh, c, xc, xs):
+            acc = accs.tile([P, 4, P], F32, name="acc", tag="acc")
+            hs = slice(c * P, (c + 1) * P)
+            for a in range(4):
+                g = 4 * gh + a
+                ts = slice(a * 2 * P + (i % 2) * P, a * 2 * P + (i % 2) * P + P)
+                nc.tensor.matmul_mx(out=acc[:, a, :], lhsT=xc[:, ts].bitcast(FP8X4), lhsT_scale=xs[:, ts],
+                                    rhs=w_codes[:, g, hs].bitcast(FP8X4), rhs_scale=w_scales[:, g, hs],
+                                    start=True, stop=True)
+            osb = osb_of(i, c)[0]
+            nc.vector.tensor_tensor(out=osb[:, :, 4 * gh:4 * gh + 4], in0=acc[:].rearrange("p g h -> p h g"),
+                                    in1=bias_blk[:, gh, c], op=ADD)
+            finish(i, c)
+
+        def unit_b1(gh, c, xc, xs):
+            yt = work.tile([P, 4, 2 * P], F32, name="yt", tag="yt")
+            hs = slice(c * P, (c + 1) * P)
+            for m in range(2):
+                acc = accs.tile([P, 2, 2 * P], F32, name="accb", tag="acc")
+                for a in (2 * m, 2 * m + 1):
+                    g = 4 * gh + a
+                    ts = slice(a * 2 * P, (a + 1) * 2 * P)
+                    nc.tensor.matmul_mx(out=acc[:, a % 2, :], lhsT=w_codes[:, g, hs].bitcast(FP8X4),
+                                        lhsT_scale=w_scales[:, g, hs], rhs=xc[:, ts].bitcast(FP8X4),
+                                        rhs_scale=xs[:, ts], start=True, stop=True)
+                for a in (2 * m, 2 * m + 1):
+                    col = (4 * gh + a) * HC + c
+                    nc.scalar.activation(out=yt[:, a, :], in_=acc[:, a % 2, :], func=IDENT,
+                                         bias=bias_col[:, col:col + 1], scale=1.0)
+            return yt
+
+        def unit_b2(q, gh, c, yt):
+            for t in range(2):
+                bt = bts.tile([P, 4, P], F32, name="bt", tag="bt")
+                for a in range(4):
+                    nc.tensor.transpose(bt[:, a, :], yt[:, a, t * P:(t + 1) * P], ident[:])
+                osb = osb_of(2 * q + t, c)[0]
+                dst = osb[:, :, 4 * gh:4 * gh + 4]
+                src = bt[:].rearrange("p g h -> p h g")
+                if second_copy_on_vector(q, c, t):
+                    nc.vector.tensor_copy(out=dst, in_=src)
+                else:
+                    nc.scalar.copy(out=dst, in_=src)
+                finish(2 * q + t, c)
+
+        need_blk = []
+        for gh in (0, 1):
+            for c in range(HC):
+                if not all(long_way(q, gh, c) for q in range(NPAIR)):
+                    need_blk.append((gh, c))
+
+        prep_scale()
+
+        xg_of = {}
+        code_of = {}
+        wg_of = {}
+        yt_of = {}
+        for tick in range(NCH + 6):
+            if tick < NCH:
+                xb = widen(tick)
+            due = []
+            for q in range(NPAIR):
+                for gh in (1, 0):
+                    c = tick - (4 * q + 5 - 2 * gh)
+                    if 0 <= c < HC:
+                        due.append((q, gh, c))
+            for q, gh, c in due:
+                if not long_way(q, gh, c):
+                    for t in range(2):
+                        unit_a(2 * q + t, gh, c, code_of[(q, gh)][0], code_of[(q, gh)][1])
+            for q, gh, c in due:
+                if long_way(q, gh, c):
+                    yt_of[(tick, q, gh, c)] = unit_b1(gh, c, code_of[(q, gh)][0], code_of[(q, gh)][1])
+            if tick % 2 == 0 and 2 <= tick <= NCH:
+                half = ((tick - 2) // 4, 1 - ((tick - 2) % 4) // 2)
+                code_of[half] = quant_x(xg_of[half])
+            if WT0 <= tick < WT0 + 4:
+                for g in W_ORDER[2 * (tick - WT0):2 * (tick - WT0) + 2]:
+                    wg_of[g] = turn_w(g)
+            if tick < NCH:
+                half = (tick // 4, 1 - (tick % 4) // 2)
+                if tick % 2 == 0:
+                    xg_of[half] = work.tile([P, 2 * HALF], BF16, name="xg", tag="xg", align_bytes=64, bufs=2)
+                turn_x(xb, xg_of[half], tick % 2)
+            for key in sorted(yt_of):
+                if key[0] == tick - 1:
+                    unit_b2(key[1], key[2], key[3], yt_of[key])
+            if tick == 0:
+                prep_bias_col()
+            for key in need_blk[3 * tick:3 * tick + 3]:
+                prep_bias_blk(key[0], key[1])
+            if WT0 <= tick < WT0 + 4:
+                for g in W_ORDER[2 * (tick - WT0):2 * (tick - WT0) + 2]:
+                    quant_w(g, wg_of[g])

@@ -26,7 +26,7 @@ HALF = 4 * I
 
 FLOPS = 2 * NTOK * G * I * H
 
-WT0 = 1
+WT0 = 0
 W_ORDER = (4, 5, 6, 7, 0, 1, 2, 3)
 
 
@@ -50,10 +50,9 @@ def tile_groupedlinear_kernel(tc, x_bytes, x_scale, W, b, out):
         work = ctx.enter_context(tc.tile_pool(name="work", bufs=3))
         codes = ctx.enter_context(tc.tile_pool(name="codes", bufs=4))
         outp = ctx.enter_context(tc.tile_pool(name="outp", bufs=8))
-        tps = ctx.enter_context(tc.psum_pool(name="tps", bufs=2))
-        accs = ctx.enter_context(tc.psum_pool(name="accs", bufs=4))
-        bts = ctx.enter_context(tc.psum_pool(name="bts", bufs=2))
-        ctx.enter_context(tc.manual_schedule(engines={mybir.EngineType.PE}))
+        vps = ctx.enter_context(tc.psum_pool(name="vps", bufs=4))
+        sps = ctx.enter_context(tc.psum_pool(name="sps", bufs=4))
+        ctx.enter_context(tc.manual_schedule(engines={mybir.EngineType.PE, mybir.EngineType.SP}))
 
         srow = const.tile([P, P], F32, name="srow")
         nc.gpsimd.memset(srow[:], 0.0)
@@ -73,9 +72,11 @@ def tile_groupedlinear_kernel(tc, x_bytes, x_scale, W, b, out):
         w_raw = const.tile([P, G, HC, I], BF16, name="w_raw")
         for i in range(2):
             nc.sync.dma_start(out=xbytes[i][:, HALF:2 * HALF], in_=xb_flat[i * P:(i + 1) * P, HALF:2 * HALF])
+        for g in W_ORDER[0:2]:
+            nc.sync.dma_start(out=w_raw[:, g], in_=W[g].rearrange("(c p) k -> p c k", p=P))
         for i in range(2):
             nc.sync.dma_start(out=xbytes[i][:, 0:HALF], in_=xb_flat[i * P:(i + 1) * P, 0:HALF])
-        for g in W_ORDER:
+        for g in W_ORDER[2:]:
             nc.sync.dma_start(out=w_raw[:, g], in_=W[g].rearrange("(c p) k -> p c k", p=P))
         for i in range(2, NT):
             nc.sync.dma_start(out=xbytes[i][:], in_=xb_flat[i * P:(i + 1) * P, :])
@@ -83,15 +84,15 @@ def tile_groupedlinear_kernel(tc, x_bytes, x_scale, W, b, out):
         w_codes = const.tile([P, G, H], U32, name="w_codes", align_bytes=64)
         w_scales = const.tile([P, G, H], U8, name="w_scales", align_bytes=64)
         bias_col = const.tile([P, G * HC], F32, name="bias_col")
-        bias_blk = const.tile([P, 2, HC, P, 4], F32, name="bias_blk")
+        bias_blk = const.tile([P, 1, HC, P, 4], F32, name="bias_blk")
 
         def prep_scale():
-            pst = tps.tile([P, P], F32, name="pst", tag="tp")
+            pst = sps.tile([P, P], F32, name="pst", tag="s")
             nc.tensor.transpose(pst[:], srow[:], ident[:])
             scol = const.tile([P, G * I // P], F32, name="scol")
             nc.vector.tensor_copy(out=scol[:], in_=pst[:, 0:G * I // P])
             for n, bank in enumerate((4, 5, 6, 7, 0, 1, 2, 3)):
-                pbc = accs.tile([P, 4, P], F32, name="pbc", tag="acc")
+                pbc = vps.tile([P, 4, P], F32, name="pbc", tag="v")
                 for j in range(4 * bank, 4 * bank + 4):
                     nc.tensor.transpose(pbc[:, j % 4, :], scol[:, j:j + 1].to_broadcast([P, P]), ident[:])
                 dst = scale_bc[:, bank * I:(bank + 1) * I]
@@ -101,17 +102,17 @@ def tile_groupedlinear_kernel(tc, x_bytes, x_scale, W, b, out):
                     nc.scalar.copy(out=dst, in_=pbc[:].rearrange("p q n -> p (q n)"))
 
         def prep_bias_col():
-            pb = tps.tile([P, P], BF16, name="pb", tag="tp")
+            pb = sps.tile([P, P], BF16, name="pb", tag="s")
             nc.tensor.transpose(pb[:], brow[:], ident_bf[:])
             nc.scalar.copy(out=bias_col[:], in_=pb[:, 0:G * HC])
 
         def prep_bias_blk(gh, c):
-            ps = accs.tile([P, 4, P], F32, name="ps", tag="acc")
+            ps = vps.tile([P, 4, P], F32, name="ps", tag="v")
             for a in range(4):
                 row = (4 * gh + a) * HC + c
                 nc.tensor.matmul(out=ps[:, a, :], lhsT=ident_bf[:, row:row + 1].to_broadcast([P, P]), rhs=brow[:],
                                  start=True, stop=True)
-            nc.scalar.copy(out=bias_blk[:, gh, c], in_=ps[:].rearrange("p a h -> p h a"))
+            nc.vector.tensor_copy(out=bias_blk[:, gh, c], in_=ps[:].rearrange("p a h -> p h a"))
 
         def widen(k):
             q, r = k // 4, k % 4
@@ -125,9 +126,14 @@ def tile_groupedlinear_kernel(tc, x_bytes, x_scale, W, b, out):
                                         in1=scale_bc[:, cs], op=MULT)
             return xb
 
-        def turn(words, dst_words):
+        def turn(words, dst_words, spare_banks=False):
             for j in range(2):
-                tp = tps.tile([P, 2, 2, P], F32, name="tp", tag="tp")
+                if not spare_banks:
+                    tp = sps.tile([P, 2, 2, P], F32, name="tp", tag="s")
+                elif j == 0:
+                    tp = vps.tile([P, 2, 2, P], F32, name="tpa", tag="v")
+                else:
+                    tp = sps.tile([P, 2, 2, P], F32, name="tpb", tag="s")
                 for a in range(2):
                     n = 2 * j + a
                     for u in range(2):
@@ -144,14 +150,17 @@ def tile_groupedlinear_kernel(tc, x_bytes, x_scale, W, b, out):
             nc.vector.quantize_mx(out=xc[:].bitcast(FP8X4), scales=xs[:], in_=xg[:])
             return xc, xs
 
-        def turn_w(g):
-            wg = work.tile([P, H * 4], BF16, name="wg", tag="wg", align_bytes=64, bufs=2)
-            turn(w_raw[:, g].rearrange("p c k -> p (c k)").bitcast(F32),
-                 wg[:].bitcast(F32).rearrange("p (a r u) -> p a r u", a=4, u=2))
+        def turn_w(g0):
+            wg = work.tile([P, 2, H * 4], BF16, name="wg", tag="wg", align_bytes=64, bufs=2)
+            for n in range(2):
+                turn(w_raw[:, g0 + n].rearrange("p c k -> p (c k)").bitcast(F32),
+                     wg[:, n].bitcast(F32).rearrange("p (a r u) -> p a r u", a=4, u=2), spare_banks=True)
             return wg
 
-        def quant_w(g, wg):
-            nc.vector.quantize_mx(out=w_codes[:, g].bitcast(FP8X4), scales=w_scales[:, g], in_=wg[:])
+        def quant_w(g0, wg):
+            nc.vector.quantize_mx(out=w_codes[:, g0:g0 + 2].rearrange("p g h -> p (g h)").bitcast(FP8X4),
+                                  scales=w_scales[:, g0:g0 + 2].rearrange("p g h -> p (g h)"),
+                                  in_=wg[:].rearrange("p g n -> p (g n)"))
 
         osbs = {}
 
@@ -168,7 +177,7 @@ def tile_groupedlinear_kernel(tc, x_bytes, x_scale, W, b, out):
                                   in_=ent[0][:].rearrange("p h g -> p (h g)"))
 
         def unit_a(i, gh, c, xc, xs):
-            acc = accs.tile([P, 4, P], F32, name="acc", tag="acc")
+            acc = vps.tile([P, 4, P], F32, name="acc", tag="v")
             hs = slice(c * P, (c + 1) * P)
             for a in range(4):
                 g = 4 * gh + a
@@ -185,7 +194,7 @@ def tile_groupedlinear_kernel(tc, x_bytes, x_scale, W, b, out):
             yt = work.tile([P, 4, 2 * P], F32, name="yt", tag="yt")
             hs = slice(c * P, (c + 1) * P)
             for m in range(2):
-                acc = accs.tile([P, 2, 2 * P], F32, name="accb", tag="acc")
+                acc = sps.tile([P, 2, 2 * P], F32, name="accb", tag="s")
                 for a in (2 * m, 2 * m + 1):
                     g = 4 * gh + a
                     ts = slice(a * 2 * P, (a + 1) * 2 * P)
@@ -200,7 +209,7 @@ def tile_groupedlinear_kernel(tc, x_bytes, x_scale, W, b, out):
 
         def unit_b2(q, gh, c, yt):
             for t in range(2):
-                bt = bts.tile([P, 4, P], F32, name="bt", tag="bt")
+                bt = sps.tile([P, 4, P], F32, name="bt", tag="s")
                 for a in range(4):
                     nc.tensor.transpose(bt[:, a, :], yt[:, a, t * P:(t + 1) * P], ident[:])
                 osb = osb_of(2 * q + t, c)[0]
@@ -244,8 +253,8 @@ def tile_groupedlinear_kernel(tc, x_bytes, x_scale, W, b, out):
                 half = ((tick - 2) // 4, 1 - ((tick - 2) % 4) // 2)
                 code_of[half] = quant_x(xg_of[half])
             if WT0 <= tick < WT0 + 4:
-                for g in W_ORDER[2 * (tick - WT0):2 * (tick - WT0) + 2]:
-                    wg_of[g] = turn_w(g)
+                g0 = W_ORDER[2 * (tick - WT0)]
+                wg_of[g0] = turn_w(g0)
             if tick < NCH:
                 half = (tick // 4, 1 - (tick % 4) // 2)
                 if tick % 2 == 0:
@@ -259,5 +268,5 @@ def tile_groupedlinear_kernel(tc, x_bytes, x_scale, W, b, out):
             for key in need_blk[3 * tick:3 * tick + 3]:
                 prep_bias_blk(key[0], key[1])
             if WT0 <= tick < WT0 + 4:
-                for g in W_ORDER[2 * (tick - WT0):2 * (tick - WT0) + 2]:
-                    quant_w(g, wg_of[g])
+                g0 = W_ORDER[2 * (tick - WT0)]
+                quant_w(g0, wg_of[g0])

@@ -91,15 +91,15 @@ def tile_groupedlinear_kernel(tc, x_bytes, x_scale, W, b, out):
             nc.tensor.transpose(pst[:], srow[:], ident[:])
             scol = const.tile([P, G * I // P], F32, name="scol")
             nc.vector.tensor_copy(out=scol[:], in_=pst[:, 0:G * I // P])
+            prep_bias_col()
+            for c in range(HC):
+                prep_bias_blk(0, c)
             for n, bank in enumerate((4, 5, 6, 7, 0, 1, 2, 3)):
                 pbc = vps.tile([P, 4, P], F32, name="pbc", tag="v")
                 for j in range(4 * bank, 4 * bank + 4):
                     nc.tensor.transpose(pbc[:, j % 4, :], scol[:, j:j + 1].to_broadcast([P, P]), ident[:])
                 dst = scale_bc[:, bank * I:(bank + 1) * I]
-                if n in (0, 1):
-                    nc.vector.tensor_copy(out=dst, in_=pbc[:].rearrange("p q n -> p (q n)"))
-                else:
-                    nc.scalar.copy(out=dst, in_=pbc[:].rearrange("p q n -> p (q n)"))
+                nc.scalar.copy(out=dst, in_=pbc[:].rearrange("p q n -> p (q n)"))
 
         def prep_bias_col():
             pb = sps.tile([P, P], BF16, name="pb", tag="s")
@@ -107,7 +107,7 @@ def tile_groupedlinear_kernel(tc, x_bytes, x_scale, W, b, out):
             nc.scalar.copy(out=bias_col[:], in_=pb[:, 0:G * HC])
 
         def prep_bias_blk(gh, c):
-            ps = vps.tile([P, 4, P], F32, name="ps", tag="v")
+            ps = sps.tile([P, 4, P], F32, name="ps", tag="s")
             for a in range(4):
                 row = (4 * gh + a) * HC + c
                 nc.tensor.matmul(out=ps[:, a, :], lhsT=ident_bf[:, row:row + 1].to_broadcast([P, P]), rhs=brow[:],
@@ -263,10 +263,6 @@ def tile_groupedlinear_kernel(tc, x_bytes, x_scale, W, b, out):
             for key in sorted(yt_of):
                 if key[0] == tick - 1:
                     unit_b2(key[1], key[2], key[3], yt_of[key])
-            if tick == 0:
-                prep_bias_col()
-            for key in need_blk[3 * tick:3 * tick + 3]:
-                prep_bias_blk(key[0], key[1])
             if WT0 <= tick < WT0 + 4:
                 g0 = W_ORDER[2 * (tick - WT0)]
                 quant_w(g0, wg_of[g0])

from contextlib import ExitStack

import concourse.mybir as mybir
from concourse.masks import make_identity

F32 = mybir.dt.float32
BF16 = mybir.dt.bfloat16
U32 = mybir.dt.uint32
U8 = mybir.dt.uint8
FP8 = mybir.dt.float8_e4m3fn
FP8X4 = mybir.dt.float8_e4m3fn_x4
MULT = mybir.AluOpType.mult
ADD = mybir.AluOpType.add
IDENT = mybir.ActivationFunctionType.Identity

P = 128
NTOK = 1024
G = 8
I = 512
H = 512
NT = NTOK // P
HC = H // P
NPAIR = NT // 2
NCH = 2 * NT
HALF = 4 * I

FLOPS = 2 * NTOK * G * I * H

WT0 = 0
W_ORDER = (4, 5, 6, 7, 0, 1, 2, 3)


def long_way(q, gh, c):
    return gh == 1


def second_copy_on_vector(q, c, t):
    return False


def tile_groupedlinear_kernel(tc, x_bytes, x_scale, W, b, out):
    nc = tc.nc
    xb_flat = x_bytes.flatten_outer_dims()
    out_flat = out.flatten_outer_dims()
    scale_row = x_scale.rearrange("a b k -> (a b k)")

    with ExitStack() as ctx:
        const = ctx.enter_context(tc.tile_pool(name="const", bufs=1))
        xin = ctx.enter_context(tc.tile_pool(name="xin", bufs=8))
        work = ctx.enter_context(tc.tile_pool(name="work", bufs=3))
        codes = ctx.enter_context(tc.tile_pool(name="codes", bufs=4))
        outp = ctx.enter_context(tc.tile_pool(name="outp", bufs=8))
        vps = ctx.enter_context(tc.psum_pool(name="vps", bufs=4))
        sps = ctx.enter_context(tc.psum_pool(name="sps", bufs=4))
        ctx.enter_context(tc.manual_schedule(engines={mybir.EngineType.PE, mybir.EngineType.SP}))

        srow = const.tile([P, P], F32, name="srow")
        nc.gpsimd.memset(srow[:], 0.0)
        nc.sync.dma_start(out=srow[0:G * I // P, :], in_=scale_row.rearrange("(j i) -> j i", i=P))
        ident = const.tile([P, P], F32, name="ident")
        make_identity(nc, ident[:])
        brow = const.tile([P, P], BF16, name="brow")
        nc.gpsimd.memset(brow[:], 0.0)
        nc.scalar.dma_start(out=brow[0:G * HC, :], in_=b.rearrange("g (c p) -> (g c) p", p=P))
        ident_bf = const.tile([P, P], BF16, name="ident_bf")
        make_identity(nc, ident_bf[:])

        xbytes = []
        for i in range(NT):
            xbytes.append(xin.tile([P, G * I], U8, name="xbytes%d" % i, tag="xbytes"))
        scale_bc = const.tile([P, G * I], F32, name="scale_bc")
        w_raw = const.tile([P, G, HC, I], BF16, name="w_raw")
        for i in range(2):
            nc.sync.dma_start(out=xbytes[i][:, HALF:2 * HALF], in_=xb_flat[i * P:(i + 1) * P, HALF:2 * HALF])
        for g in W_ORDER[0:2]:
            nc.sync.dma_start(out=w_raw[:, g], in_=W[g].rearrange("(c p) k -> p c k", p=P))
        for i in range(2):
            nc.sync.dma_start(out=xbytes[i][:, 0:HALF], in_=xb_flat[i * P:(i + 1) * P, 0:HALF])
        for g in W_ORDER[2:]:
            nc.sync.dma_start(out=w_raw[:, g], in_=W[g].rearrange("(c p) k -> p c k", p=P))
        for i in range(2, NT):
            nc.sync.dma_start(out=xbytes[i][:], in_=xb_flat[i * P:(i + 1) * P, :])

        w_codes = const.tile([P, G, H], U32, name="w_codes", align_bytes=64)
        w_scales = const.tile([P, G, H], U8, name="w_scales", align_bytes=64)
        bias_col = const.tile([P, G * HC], F32, name="bias_col")
        bias_blk = const.tile([P, 1, HC, P, 4], F32, name="bias_blk")

        def prep_scale():
            pst = sps.tile([P, P], F32, name="pst", tag="s")
            nc.tensor.transpose(pst[:], srow[:], ident[:])
            scol = const.tile([P, G * I // P], F32, name="scol")
            nc.vector.tensor_copy(out=scol[:], in_=pst[:, 0:G * I // P])
            prep_bias_col()
            for c in range(HC):
                prep_bias_blk(0, c)
            for n, bank in enumerate((4, 5, 6, 7, 0, 1, 2, 3)):
                pbc = vps.tile([P, 4, P], F32, name="pbc", tag="v")
                for j in range(4 * bank, 4 * bank + 4):
                    nc.tensor.transpose(pbc[:, j % 4, :], scol[:, j:j + 1].to_broadcast([P, P]), ident[:])
                dst = scale_bc[:, bank * I:(bank + 1) * I]
                nc.scalar.copy(out=dst, in_=pbc[:].rearrange("p q n -> p (q n)"))

        def prep_bias_col():
            pb = sps.tile([P, P], BF16, name="pb", tag="s")
            nc.tensor.transpose(pb[:], brow[:], ident_bf[:])
            nc.scalar.copy(out=bias_col[:], in_=pb[:, 0:G * HC])

        def prep_bias_blk(gh, c):
            ps = sps.tile([P, 4, P], F32, name="ps", tag="s")
            for a in range(4):
                row = (4 * gh + a) * HC + c
                nc.tensor.matmul(out=ps[:, a, :], lhsT=ident_bf[:, row:row + 1].to_broadcast([P, P]), rhs=brow[:],
                                 start=True, stop=True)
            nc.vector.tensor_copy(out=bias_blk[:, gh, c], in_=ps[:].rearrange("p a h -> p h a"))

        def widen(k):
            q, r = k // 4, k % 4
            i, gh = 2 * q + r % 2, 1 - r // 2
            xb = work.tile([P, HALF], BF16, name="xb", tag="xb")
            pieces = 2 if k == 0 else 1
            w = HALF // pieces
            for n in range(pieces):
                cs = slice(gh * HALF + n * w, gh * HALF + (n + 1) * w)
                nc.vector.tensor_tensor(out=xb[:, n * w:(n + 1) * w], in0=xbytes[i][:, cs].bitcast(FP8),
                                        in1=scale_bc[:, cs], op=MULT)
            return xb

        def turn(words, dst_words, spare_banks=False):
            for j in range(2):
                if not spare_banks:
                    tp = sps.tile([P, 2, 2, P], F32, name="tp", tag="s")
                elif j == 0:
                    tp = vps.tile([P, 2, 2, P], F32, name="tpa", tag="v")
                else:
                    tp = sps.tile([P, 2, 2, P], F32, name="tpb", tag="s")
                for a in range(2):
                    n = 2 * j + a
                    for u in range(2):
                        nc.tensor.transpose(tp[:, a, u, :], words[:, 256 * n + u:256 * (n + 1):2], ident[:])
                nc.scalar.copy(out=dst_words[:, 2 * j:2 * j + 2], in_=tp[:].rearrange("p a u r -> p a r u"))

        def turn_x(xb, xg, t):
            xg_words = xg[:].bitcast(F32).rearrange("p (a r u) -> p a r u", a=4, u=2)
            turn(xb[:].bitcast(F32), xg_words[:, :, t * P:(t + 1) * P, :])

        def quant_x(xg):
            xc = codes.tile([P, 8 * P], U32, name="xc", tag="xc", align_bytes=64)
            xs = codes.tile([P, 8 * P], U8, name="xs", tag="xs", align_bytes=64)
            nc.vector.quantize_mx(out=xc[:].bitcast(FP8X4), scales=xs[:], in_=xg[:])
            return xc, xs

        def turn_w(g0):
            wg = work.tile([P, 2, H * 4], BF16, name="wg", tag="wg", align_bytes=64, bufs=2)
            for n in range(2):
                turn(w_raw[:, g0 + n].rearrange("p c k -> p (c k)").bitcast(F32),
                     wg[:, n].bitcast(F32).rearrange("p (a r u) -> p a r u", a=4, u=2), spare_banks=True)
            return wg

        def quant_w(g0, wg):
            nc.vector.quantize_mx(out=w_codes[:, g0:g0 + 2].rearrange("p g h -> p (g h)").bitcast(FP8X4),
                                  scales=w_scales[:, g0:g0 + 2].rearrange("p g h -> p (g h)"),
                                  in_=wg[:].rearrange("p g n -> p (g n)"))

        osbs = {}

        def osb_of(i, c):
            if (i, c) not in osbs:
                osbs[(i, c)] = [outp.tile([P, P, G], F32, name="osb", tag="osb"), 0]
            return osbs[(i, c)]

        def finish(i, c):
            ent = osb_of(i, c)
            ent[1] += 1
            if ent[1] == 2:
                nc.sync.dma_start(out=out_flat[i * P:(i + 1) * P, c * P * G:(c + 1) * P * G],
                                  in_=ent[0][:].rearrange("p h g -> p (h g)"))

        def unit_a(i, gh, c, xc, xs):
            acc = vps.tile([P, 4, P], F32, name="acc", tag="v")
            hs = slice(c * P, (c + 1) * P)
            for a in range(4):
                g = 4 * gh + a
                ts = slice(a * 2 * P + (i % 2) * P, a * 2 * P + (i % 2) * P + P)
                nc.tensor.matmul_mx(out=acc[:, a, :], lhsT=xc[:, ts].bitcast(FP8X4), lhsT_scale=xs[:, ts],
                                    rhs=w_codes[:, g, hs].bitcast(FP8X4), rhs_scale=w_scales[:, g, hs],
                                    start=True, stop=True)
            osb = osb_of(i, c)[0]
            nc.vector.tensor_tensor(out=osb[:, :, 4 * gh:4 * gh + 4], in0=acc[:].rearrange("p g h -> p h g"),
                                    in1=bias_blk[:, gh, c], op=ADD)
            finish(i, c)

        def unit_b1(gh, c, xc, xs):
            yt = work.tile([P, 4, 2 * P], F32, name="yt", tag="yt")
            hs = slice(c * P, (c + 1) * P)
            for m in range(2):
                acc = sps.tile([P, 2, 2 * P], F32, name="accb", tag="s")
                for a in (2 * m, 2 * m + 1):
                    g = 4 * gh + a
                    ts = slice(a * 2 * P, (a + 1) * 2 * P)
                    nc.tensor.matmul_mx(out=acc[:, a % 2, :], lhsT=w_codes[:, g, hs].bitcast(FP8X4),
                                        lhsT_scale=w_scales[:, g, hs], rhs=xc[:, ts].bitcast(FP8X4),
                                        rhs_scale=xs[:, ts], start=True, stop=True)
                for a in (2 * m, 2 * m + 1):
                    col = (4 * gh + a) * HC + c
                    nc.scalar.activation(out=yt[:, a, :], in_=acc[:, a % 2, :], func=IDENT,
                                         bias=bias_col[:, col:col + 1], scale=1.0)
            return yt

        def unit_b2(q, gh, c, yt):
            for t in range(2):
                bt = sps.tile([P, 4, P], F32, name="bt", tag="s")
                for a in range(4):
                    nc.tensor.transpose(bt[:, a, :], yt[:, a, t * P:(t + 1) * P], ident[:])
                osb = osb_of(2 * q + t, c)[0]
                dst = osb[:, :, 4 * gh:4 * gh + 4]
                src = bt[:].rearrange("p g h -> p h g")
                if second_copy_on_vector(q, c, t):
                    nc.vector.tensor_copy(out=dst, in_=src)
                else:
                    nc.scalar.copy(out=dst, in_=src)
                finish(2 * q + t, c)

        need_blk = []
        for gh in (0, 1):
            for c in range(HC):
                if not all(long_way(q, gh, c) for q in range(NPAIR)):
                    need_blk.append((gh, c))

        prep_scale()

        xg_of = {}
        code_of = {}
        wg_of = {}
        yt_of = {}
        for tick in range(NCH + 6):
            if tick < NCH:
                xb = widen(tick)
            due = []
            for q in range(NPAIR):
                for gh in (1, 0):
                    c = tick - (4 * q + 5 - 2 * gh)
                    if 0 <= c < HC:
                        due.append((q, gh, c))
            for q, gh, c in due:
                if not long_way(q, gh, c):
                    for t in range(2):
                        unit_a(2 * q + t, gh, c, code_of[(q, gh)][0], code_of[(q, gh)][1])
            for q, gh, c in due:
                if long_way(q, gh, c):
                    yt_of[(tick, q, gh, c)] = unit_b1(gh, c, code_of[(q, gh)][0], code_of[(q, gh)][1])
            if tick % 2 == 0 and 2 <= tick <= NCH:
                half = ((tick - 2) // 4, 1 - ((tick - 2) % 4) // 2)
                code_of[half] = quant_x(xg_of[half])
            if WT0 <= tick < WT0 + 4:
                g0 = W_ORDER[2 * (tick - WT0)]
                wg_of[g0] = turn_w(g0)
            if tick < NCH:
                half = (tick // 4, 1 - (tick % 4) // 2)
                if tick % 2 == 0:
                    xg_of[half] = work.tile([P, 2 * HALF], BF16, name="xg", tag="xg", align_bytes=64, bufs=2)
                turn_x(xb, xg_of[half], tick % 2)
            for key in sorted(yt_of):
                if key[0] == tick - 1:
                    unit_b2(key[1], key[2], key[3], yt_of[key])
            if WT0 <= tick < WT0 + 4:
                g0 = W_ORDER[2 * (tick - WT0)]
                quant_w(g0, wg_of[g0])
